import numpy as np
import ml_dtypes


def mxq(x, axis, fmt="e4m3"):
    dtype, down = {"e4m3": (ml_dtypes.float8_e4m3fn, 7), "e5m2": (ml_dtypes.float8_e5m2, 14)}[fmt]
    v = np.moveaxis(np.asarray(x, np.float32).astype(ml_dtypes.bfloat16).astype(np.float64), axis, -1)
    blocks = v.reshape(v.shape[:-1] + (-1, 32))
    amax = np.abs(blocks).max(-1, keepdims=True)
    byte = np.maximum(np.where(amax > 0, np.frexp(amax)[1] - 1 + 127, 0) - down, 1)
    scale = np.exp2(byte - 127.0)
    codes = (blocks / scale).astype(np.float32).astype(dtype).astype(np.float64)
    return np.moveaxis((codes * scale).reshape(v.shape), -1, axis)


WIDE = False


def mx_kscale(k):
    if not WIDE:
        return np.ones(k)
    levels = np.array([10, -10, 5, -5, 0])
    if k % 512:
        return np.exp2(np.random.permutation(np.resize(levels, k // 32))).repeat(32)
    a = np.empty((k // 512, 16))
    for p in range(k // 512):
        a[p, :8] = np.random.permutation(np.resize(levels, 8))
        for g in range(8):
            far = levels[np.abs(levels - a[p, g]) >= 10]
            a[p, g + 8] = far[np.random.randint(len(far))]
    return np.exp2(a.ravel()).repeat(32)


BF16 = ml_dtypes.bfloat16


def bf(x):
    return np.asarray(x, np.float32).astype(BF16)


def f64(x):
    return np.asarray(x).astype(np.float64)


N, D, HOP = 4096, 128, 2
NW = HOP + 1


def setup_inputs():
    s = mx_kscale(N)
    u = s / s.min()
    g = u[None, :] / u[:, None]
    return {"A_p": bf(np.random.standard_normal((N, N)) / np.sqrt(N) * g),
            "x_p": bf(np.random.standard_normal((N, D)) / u[:, None]),
            "w_p": bf(1.0 + 0.1 * np.random.standard_normal((NW, 1)))}


def reference(A_p, x_p, w_p):
    ap = mxq(f64(A_p), 1, "e4m3")
    x = f64(x_p)
    wa, wb, wc = f64(w_p)
    feat_p = wa * x
    h1 = ap @ mxq(x, 0, "e4m3")
    feat_p = feat_p + wb * h1
    feat_p = feat_p + wc * (ap @ mxq(h1, 0, "e4m3"))
    return feat_p

@@ -1,0 +1,224 @@
+from contextlib import ExitStack
+
+import concourse.masks as masks
+import concourse.mybir as mybir
+
+F32 = mybir.dt.float32
+BF16 = mybir.dt.bfloat16
+U32 = mybir.dt.uint32
+U8 = mybir.dt.uint8
+FP8X4 = mybir.dt.float8_e4m3fn_x4
+ALU = mybir.AluOpType
+ACT = mybir.ActivationFunctionType
+
+P = 128
+NODES = 4096
+FEATURES = 128
+PASSES = NODES // (4 * P)
+ROW_TILES = NODES // P
+PAIRS = ROW_TILES // 2
+BANK = 512
+TILE_WORDS = PASSES * P
+TRANSPOSE_BANKS = 6
+RAW_TILES = 6
+FLOPS = 2 * 2 * NODES * NODES * FEATURES
+
+
+def h1_groups_ready(r):
+    return max(0, (r - 2) // 4)
+
+
+def tile_simpa_pb_t_kernel(tc, A_p, x_p, w_p, out):
+    nc = tc.nc
+    a_row_tiles = A_p.rearrange("(g m t) k -> g t m k", m=P, t=4)
+    out_groups = out.rearrange("(g m t) d -> g m (t d)", m=P, t=4)
+
+    with ExitStack() as ctx:
+        keep = ctx.enter_context(tc.tile_pool(name="keep", bufs=1))
+        raw_pool = ctx.enter_context(tc.tile_pool(name="raw_pool", bufs=RAW_TILES))
+        grouped_pool = ctx.enter_context(tc.tile_pool(name="grouped_pool", bufs=4))
+        h1_pool = ctx.enter_context(tc.tile_pool(name="h1_pool", bufs=2))
+        transpose_psum = ctx.enter_context(tc.psum_pool(name="transpose_psum", bufs=TRANSPOSE_BANKS))
+        product_psum = ctx.enter_context(tc.psum_pool(name="product_psum", bufs=2))
+        ctx.enter_context(tc.manual_schedule())
+
+        a_codes = keep.tile([P, ROW_TILES * TILE_WORDS], U32, name="a_codes", align_bytes=64)
+        a_scales = keep.tile([P, ROW_TILES // 4 * TILE_WORDS], U8, name="a_scales", align_bytes=64)
+        xh_codes = keep.tile([P, PASSES * 2 * FEATURES], U32, name="xh_codes", align_bytes=64)
+        xh_scales = keep.tile([P, PASSES * 2 * FEATURES], U8, name="xh_scales", align_bytes=64)
+        feat = keep.tile([P, ROW_TILES * FEATURES], F32, name="feat")
+        ident = keep.tile([P, P], F32, name="ident")
+        w_bf16 = keep.tile([P, 3], BF16, name="w_bf16")
+        w = keep.tile([P, 3], F32, name="w")
+
+        raw = {}
+        grouped = {}
+        products = {}
+        h1_grouped = {}
+        hop2 = {}
+
+        def a_plane(r, first, width):
+            g = r // 4
+            columns = ((g // 4) * 4 + r % 4) * TILE_WORDS + first
+            return a_scales[4 * (g % 4) : P, columns : columns + width]
+
+        def load(r):
+            raw[r] = raw_pool.tile([P, NODES], BF16, tag="raw", name="raw")
+            nc.sync.dma_start(out=raw[r][:], in_=a_row_tiles[r // 4][r % 4])
+
+        def quantise_a(r, half):
+            first = half * (TILE_WORDS // 2)
+            nc.vector.quantize_mx(
+                out=a_codes[:, r * TILE_WORDS + first : r * TILE_WORDS + first + TILE_WORDS // 2].bitcast(FP8X4),
+                scales=a_plane(r, first, TILE_WORDS // 2),
+                in_=grouped[(r, half)][:],
+            )
+
+        def mx_pass(acc, r, c, first, width, start):
+            moving = slice(c * 2 * FEATURES + first, c * 2 * FEATURES + first + width)
+            nc.tensor.matmul_mx(
+                out=acc,
+                lhsT=a_codes[:, r * TILE_WORDS + c * P : r * TILE_WORDS + (c + 1) * P].bitcast(FP8X4),
+                lhsT_scale=a_plane(r, c * P, P),
+                rhs=xh_codes[:, moving].bitcast(FP8X4),
+                rhs_scale=xh_scales[:, moving],
+                start=start,
+                stop=(c == PASSES - 1),
+            )
+
+        def transposes(r):
+            words = raw[r][:].bitcast(F32)
+            for b in range(4):
+                bank = transpose_psum.tile([P, BANK], F32, tag="bank", name="bank")
+                for q in range(4):
+                    nc.tensor.transpose(
+                        out=bank[:, q * P : (q + 1) * P],
+                        in_=words[:, (2 * b + q // 2) * 2 * P + q % 2 : (2 * b + q // 2 + 1) * 2 * P : 2],
+                        identity=ident[:],
+                    )
+                half = b // 2
+                if b % 2 == 0:
+                    grouped[(r, half)] = grouped_pool.tile([P, 4 * BANK], BF16, tag="grouped", name="grouped", align_bytes=64)
+                target = grouped[(r, half)][:].bitcast(F32)[:, (b % 2) * BANK : (b % 2 + 1) * BANK]
+                target = target.rearrange("p (c m u) -> p c m u", c=2, u=2)
+                source = bank[:].rearrange("p (c u m) -> p c m u", c=2, u=2)
+                if b == 3 and r % 4 != 3:
+                    nc.vector.tensor_copy(out=target, in_=source)
+                else:
+                    nc.scalar.copy(out=target, in_=source)
+                if b == 1 and r > 0:
+                    quantise_a(r - 1, 1)
+                if b == 3:
+                    quantise_a(r, 0)
+                if b == 1 and r % 2 == 0 and r >= 4:
+                    round_h1((r - 4) // 2)
+                    add_products((r - 4) // 2)
+                if b == 3 and r % 4 == 2 and r >= 6:
+                    quantise_h1((r - 6) // 4)
+
+        def hop1(r):
+            if r % 2 == 0:
+                products[r // 2] = product_psum.tile([P, BANK], F32, tag="products", name="products")
+            for c in range(PASSES):
+                width = 2 * FEATURES if c < h1_groups_ready(r) else FEATURES
+                first = (r % 2) * 2 * FEATURES
+                mx_pass(products[r // 2][:, first : first + width], r, c, 0, width, c == 0)
+
+        def round_h1(pair):
+            g = pair // 2
+            u = pair % 2
+            if u == 0:
+                h1_grouped[g] = h1_pool.tile([P, 4 * FEATURES], BF16, tag="h1", name="h1", align_bytes=64)
+            parts = products[pair][:].rearrange("p (e s d) -> p e s d", e=2, s=2)
+            nc.scalar.copy(
+                out=h1_grouped[g][:].rearrange("p (d t) -> p d t", t=4)[:, :, 2 * u : 2 * u + 2],
+                in_=parts[:, :, 0, :].rearrange("p e d -> p d e"),
+            )
+
+        def add_products(pair):
+            parts = products[pair][:].rearrange("p (e s d) -> p e s d", e=2, s=2)
+            rows = feat[:, 2 * pair * FEATURES : (2 * pair + 2) * FEATURES].rearrange("p (e d) -> p e d", e=2)
+            nc.vector.scalar_tensor_tensor(
+                out=rows, in0=parts[:, :, 0, :], scalar=w[:, 1:2], in1=rows, op0=ALU.mult, op1=ALU.add
+            )
+            if h1_groups_ready(2 * pair) > 0:
+                nc.vector.scalar_tensor_tensor(
+                    out=rows, in0=parts[:, :, 1, :], scalar=w[:, 2:3], in1=rows, op0=ALU.mult, op1=ALU.add
+                )
+
+        def quantise_h1(g):
+            columns = slice(g * 2 * FEATURES + FEATURES, (g + 1) * 2 * FEATURES)
+            nc.vector.quantize_mx(
+                out=xh_codes[:, columns].bitcast(FP8X4), scales=xh_scales[:, columns], in_=h1_grouped[g][:]
+            )
+
+        def hop2_passes(r, first_pass, last_pass):
+            g = r // 4
+            if g not in hop2:
+                if g < TRANSPOSE_BANKS:
+                    hop2[g] = transpose_psum.tile([P, BANK], F32, tag="bank", name="hop2")
+                else:
+                    hop2[g] = product_psum.tile([P, BANK], F32, tag="products", name="hop2")
+            for c in range(first_pass, last_pass + 1):
+                acc = hop2[g][:, (r % 4) * FEATURES : (r % 4 + 1) * FEATURES]
+                mx_pass(acc, r, c, FEATURES, FEATURES, c == h1_groups_ready(r))
+
+        nc.scalar.dma_start(out=w_bf16[:], in_=w_p.rearrange("a b -> (a b)").partition_broadcast(P))
+        x_raw = raw_pool.tile([P, ROW_TILES * FEATURES], BF16, tag="raw", name="x_raw")
+        nc.sync.dma_start(
+            out=x_raw[:].rearrange("p (c w) -> p c w", c=PASSES),
+            in_=x_p.rearrange("(c m t) d -> m c (t d)", m=P, t=4),
+        )
+        for r in range(RAW_TILES - 1):
+            load(r)
+        masks.make_identity(nc, ident[:])
+        nc.vector.tensor_copy(out=w[:], in_=w_bf16[:])
+        x_grouped = []
+        for half in range(2):
+            x_half = grouped_pool.tile([P, 4 * BANK], BF16, tag="grouped", name="x_half", align_bytes=64)
+            x_grouped.append(x_half)
+            nc.vector.tensor_copy(
+                out=x_half[:].rearrange("p (c d t) -> p c d t", c=4, t=4),
+                in_=x_raw[:, half * 4 * BANK : (half + 1) * 4 * BANK].rearrange("p (c t d) -> p c d t", c=4, t=4),
+            )
+        for c in range(PASSES):
+            columns = slice(c * 2 * FEATURES, c * 2 * FEATURES + FEATURES)
+            nc.vector.quantize_mx(
+                out=xh_codes[:, columns].bitcast(FP8X4),
+                scales=xh_scales[:, columns],
+                in_=x_grouped[c // 4][:, (c % 4) * BANK : (c % 4 + 1) * BANK],
+            )
+        for quarter in range(4):
+            columns = slice(quarter * 2 * BANK, (quarter + 1) * 2 * BANK)
+            nc.scalar.activation(out=feat[:, columns], in_=x_raw[:, columns], func=ACT.Copy, scale=w[:, 0:1])
+
+        for r in range(ROW_TILES):
+            if r + RAW_TILES - 1 < ROW_TILES:
+                load(r + RAW_TILES - 1)
+            transposes(r)
+            if r >= 2:
+                hop1(r - 2)
+        quantise_a(ROW_TILES - 1, 1)
+
+        round_h1(PAIRS - 2)
+        add_products(PAIRS - 2)
+        hop1(ROW_TILES - 2)
+        for g in range(TRANSPOSE_BANKS // 2):
+            hop2_passes(4 * g, h1_groups_ready(4 * g), PASSES - 2)
+        hop1(ROW_TILES - 1)
+        for g in range(TRANSPOSE_BANKS // 2, TRANSPOSE_BANKS):
+            hop2_passes(4 * g, h1_groups_ready(4 * g), PASSES - 2)
+        round_h1(PAIRS - 1)
+        quantise_h1(PASSES - 1)
+        add_products(PAIRS - 1)
+        for g in range(PASSES):
+            for r in range(4 * g, 4 * g + 4):
+                if r % 4 == 0 and g < TRANSPOSE_BANKS:
+                    hop2_passes(r, PASSES - 1, PASSES - 1)
+                else:
+                    hop2_passes(r, h1_groups_ready(r), PASSES - 1)
+            rows = feat[:, g * BANK : (g + 1) * BANK]
+            nc.vector.scalar_tensor_tensor(
+                out=rows, in0=hop2[g][:], scalar=w[:, 2:3], in1=rows, op0=ALU.mult, op1=ALU.add
+            )
+            nc.sync.dma_start(out=out_groups[g], in_=rows)

@@ -20,7 +20,7 @@ PAIRS = ROW_TILES // 2
 BANK = 512
 TILE_WORDS = PASSES * P
 TRANSPOSE_BANKS = 6
-RAW_TILES = 6
+RAW_TILES = 5
 FLOPS = 2 * 2 * NODES * NODES * FEATURES
 
 
@@ -36,6 +36,7 @@ def tile_simpa_pb_t_kernel(tc, A_p, x_p, w_p, out):
     with ExitStack() as ctx:
         keep = ctx.enter_context(tc.tile_pool(name="keep", bufs=1))
         raw_pool = ctx.enter_context(tc.tile_pool(name="raw_pool", bufs=RAW_TILES))
+        split_pool = ctx.enter_context(tc.tile_pool(name="split_pool", bufs=4))
         grouped_pool = ctx.enter_context(tc.tile_pool(name="grouped_pool", bufs=4))
         h1_pool = ctx.enter_context(tc.tile_pool(name="h1_pool", bufs=2))
         transpose_psum = ctx.enter_context(tc.psum_pool(name="transpose_psum", bufs=TRANSPOSE_BANKS))
@@ -52,6 +53,7 @@ def tile_simpa_pb_t_kernel(tc, A_p, x_p, w_p, out):
         w = keep.tile([P, 3], F32, name="w")
 
         raw = {}
+        split = {}
         grouped = {}
         products = {}
         h1_grouped = {}
@@ -65,6 +67,14 @@ def tile_simpa_pb_t_kernel(tc, A_p, x_p, w_p, out):
         def load(r):
             raw[r] = raw_pool.tile([P, NODES], BF16, tag="raw", name="raw")
             nc.sync.dma_start(out=raw[r][:], in_=a_row_tiles[r // 4][r % 4])
+
+        def split_words(r, half):
+            split[(r, half)] = split_pool.tile([P, TILE_WORDS], F32, tag="split", name="split", align_bytes=64)
+            source = raw[r][:].bitcast(F32)[:, half * TILE_WORDS : (half + 1) * TILE_WORDS]
+            nc.vector.tensor_copy(
+                out=split[(r, half)][:].rearrange("p (c u m) -> p c u m", u=2, m=P),
+                in_=source.rearrange("p (c m u) -> p c u m", u=2, m=P),
+            )
 
         def quantise_a(r, half):
             first = half * (TILE_WORDS // 2)
@@ -87,13 +97,12 @@ def tile_simpa_pb_t_kernel(tc, A_p, x_p, w_p, out):
             )
 
         def transposes(r):
-            words = raw[r][:].bitcast(F32)
             for b in range(4):
                 bank = transpose_psum.tile([P, BANK], F32, tag="bank", name="bank")
                 for q in range(4):
                     nc.tensor.transpose(
                         out=bank[:, q * P : (q + 1) * P],
-                        in_=words[:, (2 * b + q // 2) * 2 * P + q % 2 : (2 * b + q // 2 + 1) * 2 * P : 2],
+                        in_=split[(r, b // 2)][:, ((b % 2) * 4 + q) * P : ((b % 2) * 4 + q + 1) * P],
                         identity=ident[:],
                     )
                 half = b // 2
@@ -102,10 +111,9 @@ def tile_simpa_pb_t_kernel(tc, A_p, x_p, w_p, out):
                 target = grouped[(r, half)][:].bitcast(F32)[:, (b % 2) * BANK : (b % 2 + 1) * BANK]
                 target = target.rearrange("p (c m u) -> p c m u", c=2, u=2)
                 source = bank[:].rearrange("p (c u m) -> p c m u", c=2, u=2)
-                if b == 3 and r % 4 != 3:
-                    nc.vector.tensor_copy(out=target, in_=source)
-                else:
-                    nc.scalar.copy(out=target, in_=source)
+                nc.scalar.copy(out=target, in_=source)
+                if b % 2 == 0 and r + 1 < ROW_TILES:
+                    split_words(r + 1, b // 2)
                 if b == 1 and r > 0:
                     quantise_a(r - 1, 1)
                 if b == 3:
@@ -188,6 +196,9 @@ def tile_simpa_pb_t_kernel(tc, A_p, x_p, w_p, out):
                 scales=xh_scales[:, columns],
                 in_=x_grouped[c // 4][:, (c % 4) * BANK : (c % 4 + 1) * BANK],
             )
+            if c == 3:
+                split_words(0, 0)
+        split_words(0, 1)
         for quarter in range(4):
             columns = slice(quarter * 2 * BANK, (quarter + 1) * 2 * BANK)
             nc.scalar.activation(out=feat[:, columns], in_=x_raw[:, columns], func=ACT.Copy, scale=w[:, 0:1])

@@ -51,6 +51,7 @@ def tile_simpa_pb_t_kernel(tc, A_p, x_p, w_p, out):
         ident = keep.tile([P, P], F32, name="ident")
         w_bf16 = keep.tile([P, 3], BF16, name="w_bf16")
         w = keep.tile([P, 3], F32, name="w")
+        zeros = keep.tile([P, BANK], BF16, name="zeros", align_bytes=64)
 
         raw = {}
         split = {}
@@ -99,6 +100,8 @@ def tile_simpa_pb_t_kernel(tc, A_p, x_p, w_p, out):
         def transposes(r):
             for b in range(4):
                 bank = transpose_psum.tile([P, BANK], F32, tag="bank", name="bank")
+                if b == 2 and h1_groups_ready(r - 2) < PASSES // 2:
+                    nc.tensor.matmul(out=bank[:], lhsT=zeros[:, :P], rhs=zeros[:], start=True, stop=True)
                 for q in range(4):
                     nc.tensor.transpose(
                         out=bank[:, q * P : (q + 1) * P],
@@ -180,6 +183,7 @@ def tile_simpa_pb_t_kernel(tc, A_p, x_p, w_p, out):
         for r in range(RAW_TILES - 1):
             load(r)
         masks.make_identity(nc, ident[:])
+        nc.gpsimd.memset(zeros[:], 0.0)
         nc.vector.tensor_copy(out=w[:], in_=w_bf16[:])
         x_grouped = []
         for half in range(2):

@@ -100,8 +100,10 @@ def tile_simpa_pb_t_kernel(tc, A_p, x_p, w_p, out):
         def transposes(r):
             for b in range(4):
                 bank = transpose_psum.tile([P, BANK], F32, tag="bank", name="bank")
-                if b == 2 and h1_groups_ready(r - 2) < PASSES // 2:
-                    nc.tensor.matmul(out=bank[:], lhsT=zeros[:, :P], rhs=zeros[:], start=True, stop=True)
+                if b == 0:
+                    ready = h1_groups_ready(r - 2)
+                    for i in range(2 if ready < 2 else 1 if ready < 6 else 0):
+                        nc.tensor.matmul(out=bank[:], lhsT=zeros[:, :P], rhs=zeros[:], start=True, stop=True)
                 for q in range(4):
                     nc.tensor.transpose(
                         out=bank[:, q * P : (q + 1) * P],
@@ -203,6 +205,9 @@ def tile_simpa_pb_t_kernel(tc, A_p, x_p, w_p, out):
             if c == 3:
                 split_words(0, 0)
         split_words(0, 1)
+        warm = product_psum.tile([P, BANK], F32, tag="products", name="warm")
+        for source in [x_raw, x_raw, x_raw, x_raw, x_grouped[0], x_grouped[0], x_grouped[1], x_grouped[1]]:
+            nc.tensor.matmul(out=warm[:], lhsT=source[:, :P], rhs=source[:, :BANK], start=True, stop=True)
         for quarter in range(4):
             columns = slice(quarter * 2 * BANK, (quarter + 1) * 2 * BANK)
             nc.scalar.activation(out=feat[:, columns], in_=x_raw[:, columns], func=ACT.Copy, scale=w[:, 0:1])

@@ -20,7 +20,7 @@ PAIRS = ROW_TILES // 2
 BANK = 512
 TILE_WORDS = PASSES * P
 TRANSPOSE_BANKS = 6
-RAW_TILES = 5
+RAW_TILES = 4
 FLOPS = 2 * 2 * NODES * NODES * FEATURES
 
 
@@ -36,7 +36,7 @@ def tile_simpa_pb_t_kernel(tc, A_p, x_p, w_p, out):
     with ExitStack() as ctx:
         keep = ctx.enter_context(tc.tile_pool(name="keep", bufs=1))
         raw_pool = ctx.enter_context(tc.tile_pool(name="raw_pool", bufs=RAW_TILES))
-        split_pool = ctx.enter_context(tc.tile_pool(name="split_pool", bufs=4))
+        split_pool = ctx.enter_context(tc.tile_pool(name="split_pool", bufs=3))
         grouped_pool = ctx.enter_context(tc.tile_pool(name="grouped_pool", bufs=4))
         h1_pool = ctx.enter_context(tc.tile_pool(name="h1_pool", bufs=2))
         transpose_psum = ctx.enter_context(tc.psum_pool(name="transpose_psum", bufs=TRANSPOSE_BANKS))
@@ -48,11 +48,10 @@ def tile_simpa_pb_t_kernel(tc, A_p, x_p, w_p, out):
         xh_codes = keep.tile([P, PASSES * 2 * FEATURES], U32, name="xh_codes", align_bytes=64)
         xh_scales = keep.tile([P, PASSES * 2 * FEATURES], U8, name="xh_scales", align_bytes=64)
         feat = keep.tile([P, ROW_TILES * FEATURES], F32, name="feat")
+        x_raw = keep.tile([P, ROW_TILES * FEATURES], BF16, name="x_raw")
         ident = keep.tile([P, P], F32, name="ident")
         w_bf16 = keep.tile([P, 3], BF16, name="w_bf16")
         w = keep.tile([P, 3], F32, name="w")
-        zeros = keep.tile([P, BANK], BF16, name="zeros", align_bytes=64)
-
         raw = {}
         split = {}
         grouped = {}
@@ -65,15 +64,18 @@ def tile_simpa_pb_t_kernel(tc, A_p, x_p, w_p, out):
             columns = ((g // 4) * 4 + r % 4) * TILE_WORDS + first
             return a_scales[4 * (g % 4) : P, columns : columns + width]
 
-        def load(r):
+        def load(r, pieces):
             raw[r] = raw_pool.tile([P, NODES], BF16, tag="raw", name="raw")
-            nc.sync.dma_start(out=raw[r][:], in_=a_row_tiles[r // 4][r % 4])
+            width = NODES // pieces
+            for i in range(pieces):
+                columns = slice(i * width, (i + 1) * width)
+                nc.sync.dma_start(out=raw[r][:, columns], in_=a_row_tiles[r // 4][r % 4][:, columns])
 
-        def split_words(r, half):
-            split[(r, half)] = split_pool.tile([P, TILE_WORDS], F32, tag="split", name="split", align_bytes=64)
-            source = raw[r][:].bitcast(F32)[:, half * TILE_WORDS : (half + 1) * TILE_WORDS]
+        def split_words(r):
+            split[r] = split_pool.tile([P, TILE_WORDS], F32, tag="split", name="split", align_bytes=64)
+            source = raw[r][:].bitcast(F32)[:, 0:TILE_WORDS]
             nc.vector.tensor_copy(
-                out=split[(r, half)][:].rearrange("p (c u m) -> p c u m", u=2, m=P),
+                out=split[r][:].rearrange("p (c u m) -> p c u m", u=2, m=P),
                 in_=source.rearrange("p (c m u) -> p c u m", u=2, m=P),
             )
 
@@ -100,14 +102,15 @@ def tile_simpa_pb_t_kernel(tc, A_p, x_p, w_p, out):
         def transposes(r):
             for b in range(4):
                 bank = transpose_psum.tile([P, BANK], F32, tag="bank", name="bank")
-                if b == 0:
-                    ready = h1_groups_ready(r - 2)
-                    for i in range(2 if ready < 2 else 1 if ready < 6 else 0):
-                        nc.tensor.matmul(out=bank[:], lhsT=zeros[:, :P], rhs=zeros[:], start=True, stop=True)
                 for q in range(4):
+                    if b < 2:
+                        words = split[r][:, (4 * b + q) * P : (4 * b + q + 1) * P]
+                    else:
+                        first = (2 * b + q // 2) * 2 * P
+                        words = raw[r][:].bitcast(F32)[:, first + q % 2 : first + 2 * P : 2]
                     nc.tensor.transpose(
                         out=bank[:, q * P : (q + 1) * P],
-                        in_=split[(r, b // 2)][:, ((b % 2) * 4 + q) * P : ((b % 2) * 4 + q + 1) * P],
+                        in_=words,
                         identity=ident[:],
                     )
                 half = b // 2
@@ -116,16 +119,23 @@ def tile_simpa_pb_t_kernel(tc, A_p, x_p, w_p, out):
                 target = grouped[(r, half)][:].bitcast(F32)[:, (b % 2) * BANK : (b % 2 + 1) * BANK]
                 target = target.rearrange("p (c m u) -> p c m u", c=2, u=2)
                 source = bank[:].rearrange("p (c u m) -> p c m u", c=2, u=2)
-                nc.scalar.copy(out=target, in_=source)
-                if b % 2 == 0 and r + 1 < ROW_TILES:
-                    split_words(r + 1, b // 2)
+                if b == 3 and r % 4 == 1:
+                    nc.vector.tensor_copy(out=target, in_=source)
+                else:
+                    nc.scalar.copy(out=target, in_=source)
+                if b == 0 and r + 1 < ROW_TILES:
+                    split_words(r + 1)
+                if r == 0 and b in (1, 2):
+                    quantise_x(b - 1)
                 if b == 1 and r > 0:
                     quantise_a(r - 1, 1)
                 if b == 3:
                     quantise_a(r, 0)
                 if b == 1 and r % 2 == 0 and r >= 4:
                     round_h1((r - 4) // 2)
-                    add_products((r - 4) // 2)
+                    add_products((r - 4) // 2, 0)
+                if b == 2 and r % 2 == 0 and r >= 4:
+                    add_products((r - 4) // 2, 1)
                 if b == 3 and r % 4 == 2 and r >= 6:
                     quantise_h1((r - 6) // 4)
 
@@ -148,15 +158,19 @@ def tile_simpa_pb_t_kernel(tc, A_p, x_p, w_p, out):
                 in_=parts[:, :, 0, :].rearrange("p e d -> p d e"),
             )
 
-        def add_products(pair):
+        def add_products(pair, part):
             parts = products[pair][:].rearrange("p (e s d) -> p e s d", e=2, s=2)
             rows = feat[:, 2 * pair * FEATURES : (2 * pair + 2) * FEATURES].rearrange("p (e d) -> p e d", e=2)
-            nc.vector.scalar_tensor_tensor(
-                out=rows, in0=parts[:, :, 0, :], scalar=w[:, 1:2], in1=rows, op0=ALU.mult, op1=ALU.add
-            )
-            if h1_groups_ready(2 * pair) > 0:
+            if part == 0:
+                nc.vector.tensor_scalar_mul(out=rows, in0=parts[:, :, 0, :], scalar1=w[:, 1:2])
+            elif h1_groups_ready(2 * pair) > 0:
                 nc.vector.scalar_tensor_tensor(
-                    out=rows, in0=parts[:, :, 1, :], scalar=w[:, 2:3], in1=rows, op0=ALU.mult, op1=ALU.add
+                    out=rows,
+                    in0=parts[:, :, 1, :],
+                    scalar=w[:, 2:3],
+                    in1=rows,
+                    op0=ALU.mult,
+                    op1=ALU.add,
                 )
 
         def quantise_h1(g):
@@ -176,52 +190,59 @@ def tile_simpa_pb_t_kernel(tc, A_p, x_p, w_p, out):
                 acc = hop2[g][:, (r % 4) * FEATURES : (r % 4 + 1) * FEATURES]
                 mx_pass(acc, r, c, FEATURES, FEATURES, c == h1_groups_ready(r))
 
-        nc.scalar.dma_start(out=w_bf16[:], in_=w_p.rearrange("a b -> (a b)").partition_broadcast(P))
-        x_raw = raw_pool.tile([P, ROW_TILES * FEATURES], BF16, tag="raw", name="x_raw")
+        x_grouped = {}
+
+        def group_x(half):
+            x_grouped[half] = grouped_pool.tile([P, 4 * BANK], BF16, tag="grouped", name="x_half", align_bytes=64)
+            nc.vector.tensor_copy(
+                out=x_grouped[half][:].rearrange("p (c d t) -> p c d t", c=4, t=4),
+                in_=x_raw[:, half * 4 * BANK : (half + 1) * 4 * BANK].rearrange("p (c t d) -> p c d t", c=4, t=4),
+            )
+
+        def quantise_x(half):
+            for c in range(4 * half, 4 * half + 4):
+                columns = slice(c * 2 * FEATURES, c * 2 * FEATURES + FEATURES)
+                nc.vector.quantize_mx(
+                    out=xh_codes[:, columns].bitcast(FP8X4),
+                    scales=xh_scales[:, columns],
+                    in_=x_grouped[half][:, (c % 4) * BANK : (c % 4 + 1) * BANK],
+                )
+
+        def add_x(g):
+            rows = feat[:, g * BANK : (g + 1) * BANK]
+            nc.vector.scalar_tensor_tensor(
+                out=rows, in0=x_raw[:, g * BANK : (g + 1) * BANK], scalar=w[:, 0:1], in1=rows, op0=ALU.mult, op1=ALU.add
+            )
+
+        load(0, 2)
         nc.sync.dma_start(
             out=x_raw[:].rearrange("p (c w) -> p c w", c=PASSES),
             in_=x_p.rearrange("(c m t) d -> m c (t d)", m=P, t=4),
         )
-        for r in range(RAW_TILES - 1):
-            load(r)
+        for r in range(1, RAW_TILES):
+            load(r, 1)
         masks.make_identity(nc, ident[:])
-        nc.gpsimd.memset(zeros[:], 0.0)
-        nc.vector.tensor_copy(out=w[:], in_=w_bf16[:])
-        x_grouped = []
-        for half in range(2):
-            x_half = grouped_pool.tile([P, 4 * BANK], BF16, tag="grouped", name="x_half", align_bytes=64)
-            x_grouped.append(x_half)
-            nc.vector.tensor_copy(
-                out=x_half[:].rearrange("p (c d t) -> p c d t", c=4, t=4),
-                in_=x_raw[:, half * 4 * BANK : (half + 1) * 4 * BANK].rearrange("p (c t d) -> p c d t", c=4, t=4),
-            )
-        for c in range(PASSES):
-            columns = slice(c * 2 * FEATURES, c * 2 * FEATURES + FEATURES)
-            nc.vector.quantize_mx(
-                out=xh_codes[:, columns].bitcast(FP8X4),
-                scales=xh_scales[:, columns],
-                in_=x_grouped[c // 4][:, (c % 4) * BANK : (c % 4 + 1) * BANK],
-            )
-            if c == 3:
-                split_words(0, 0)
-        split_words(0, 1)
-        warm = product_psum.tile([P, BANK], F32, tag="products", name="warm")
-        for source in [x_raw, x_raw, x_raw, x_raw, x_grouped[0], x_grouped[0], x_grouped[1], x_grouped[1]]:
-            nc.tensor.matmul(out=warm[:], lhsT=source[:, :P], rhs=source[:, :BANK], start=True, stop=True)
-        for quarter in range(4):
-            columns = slice(quarter * 2 * BANK, (quarter + 1) * 2 * BANK)
-            nc.scalar.activation(out=feat[:, columns], in_=x_raw[:, columns], func=ACT.Copy, scale=w[:, 0:1])
+        split_words(0)
+        group_x(0)
+        group_x(1)
 
         for r in range(ROW_TILES):
-            if r + RAW_TILES - 1 < ROW_TILES:
-                load(r + RAW_TILES - 1)
+            if r == 1:
+                nc.scalar.dma_start(out=w_bf16[:], in_=w_p.rearrange("a b -> (a b)").partition_broadcast(P))
             transposes(r)
+            if r == 2:
+                nc.vector.tensor_copy(out=w[:], in_=w_bf16[:])
+            if r + RAW_TILES < ROW_TILES:
+                load(r + RAW_TILES, 1)
             if r >= 2:
                 hop1(r - 2)
         quantise_a(ROW_TILES - 1, 1)
 
         round_h1(PAIRS - 2)
-        add_products(PAIRS - 2)
+        add_products(PAIRS - 2, 0)
+        add_products(PAIRS - 2, 1)
+        for g in range(PASSES // 2):
+            add_x(g)
         hop1(ROW_TILES - 2)
         for g in range(TRANSPOSE_BANKS // 2):
             hop2_passes(4 * g, h1_groups_ready(4 * g), PASSES - 2)
@@ -230,13 +251,16 @@ def tile_simpa_pb_t_kernel(tc, A_p, x_p, w_p, out):
             hop2_passes(4 * g, h1_groups_ready(4 * g), PASSES - 2)
         round_h1(PAIRS - 1)
         quantise_h1(PASSES - 1)
-        add_products(PAIRS - 1)
+        add_products(PAIRS - 1, 0)
+        add_products(PAIRS - 1, 1)
         for g in range(PASSES):
             for r in range(4 * g, 4 * g + 4):
                 if r % 4 == 0 and g < TRANSPOSE_BANKS:
                     hop2_passes(r, PASSES - 1, PASSES - 1)
                 else:
                     hop2_passes(r, h1_groups_ready(r), PASSES - 1)
+            if g < PASSES // 2:
+                add_x(PASSES // 2 + g)
             rows = feat[:, g * BANK : (g + 1) * BANK]
             nc.vector.scalar_tensor_tensor(
                 out=rows, in0=hop2[g][:], scalar=w[:, 2:3], in1=rows, op0=ALU.mult, op1=ALU.add

@@ -75,8 +75,8 @@ def tile_simpa_pb_t_kernel(tc, A_p, x_p, w_p, out):
             split[r] = split_pool.tile([P, TILE_WORDS], F32, tag="split", name="split", align_bytes=64)
             source = raw[r][:].bitcast(F32)[:, 0:TILE_WORDS]
             nc.vector.tensor_copy(
-                out=split[r][:].rearrange("p (c u m) -> p c u m", u=2, m=P),
-                in_=source.rearrange("p (c m u) -> p c u m", u=2, m=P),
+                out=split[r][:].rearrange("p (u m i) -> p m u i", u=2, i=4),
+                in_=source.rearrange("p (m i u) -> p m u i", u=2, i=4),
             )
 
         def quantise_a(r, half):
@@ -102,24 +102,21 @@ def tile_simpa_pb_t_kernel(tc, A_p, x_p, w_p, out):
         def transposes(r):
             for b in range(4):
                 bank = transpose_psum.tile([P, BANK], F32, tag="bank", name="bank")
-                for q in range(4):
-                    if b < 2:
-                        words = split[r][:, (4 * b + q) * P : (4 * b + q + 1) * P]
-                    else:
-                        first = (2 * b + q // 2) * 2 * P
-                        words = raw[r][:].bitcast(F32)[:, first + q % 2 : first + 2 * P : 2]
-                    nc.tensor.transpose(
-                        out=bank[:, q * P : (q + 1) * P],
-                        in_=words,
-                        identity=ident[:],
-                    )
+                for u in range(2):
+                    for c in range(2 * b, 2 * b + 2):
+                        if b < 2:
+                            words = split[r][:, (4 * u + c) * P : (4 * u + c + 1) * P]
+                        else:
+                            words = raw[r][:].bitcast(F32)[:, c * 2 * P + u : (c + 1) * 2 * P : 2]
+                        position = (2 * u + c % 2) * P
+                        nc.tensor.transpose(out=bank[:, position : position + P], in_=words, identity=ident[:])
                 half = b // 2
                 if b % 2 == 0:
                     grouped[(r, half)] = grouped_pool.tile([P, 4 * BANK], BF16, tag="grouped", name="grouped", align_bytes=64)
                 target = grouped[(r, half)][:].bitcast(F32)[:, (b % 2) * BANK : (b % 2 + 1) * BANK]
-                target = target.rearrange("p (c m u) -> p c m u", c=2, u=2)
-                source = bank[:].rearrange("p (c u m) -> p c m u", c=2, u=2)
-                if b == 3 and r % 4 == 1:
+                target = target.rearrange("p (m i u) -> p m u i", i=2, u=2)
+                source = bank[:].rearrange("p (u m i) -> p m u i", u=2, i=2)
+                if b == 3 and r % 2 == 1:
                     nc.vector.tensor_copy(out=target, in_=source)
                 else:
                     nc.scalar.copy(out=target, in_=source)

@@ -20,6 +20,7 @@ PAIRS = ROW_TILES // 2
 BANK = 512
 TILE_WORDS = PASSES * P
 TRANSPOSE_BANKS = 6
+SPLIT_BANKS = 3
 RAW_TILES = 4
 FLOPS = 2 * 2 * NODES * NODES * FEATURES
 
@@ -36,7 +37,7 @@ def tile_simpa_pb_t_kernel(tc, A_p, x_p, w_p, out):
     with ExitStack() as ctx:
         keep = ctx.enter_context(tc.tile_pool(name="keep", bufs=1))
         raw_pool = ctx.enter_context(tc.tile_pool(name="raw_pool", bufs=RAW_TILES))
-        split_pool = ctx.enter_context(tc.tile_pool(name="split_pool", bufs=3))
+        split_pool = ctx.enter_context(tc.tile_pool(name="split_pool", bufs=2))
         grouped_pool = ctx.enter_context(tc.tile_pool(name="grouped_pool", bufs=4))
         h1_pool = ctx.enter_context(tc.tile_pool(name="h1_pool", bufs=2))
         transpose_psum = ctx.enter_context(tc.psum_pool(name="transpose_psum", bufs=TRANSPOSE_BANKS))
@@ -72,8 +73,8 @@ def tile_simpa_pb_t_kernel(tc, A_p, x_p, w_p, out):
                 nc.sync.dma_start(out=raw[r][:, columns], in_=a_row_tiles[r // 4][r % 4][:, columns])
 
         def split_words(r):
-            split[r] = split_pool.tile([P, TILE_WORDS], F32, tag="split", name="split", align_bytes=64)
-            source = raw[r][:].bitcast(F32)[:, 0:TILE_WORDS]
+            split[r] = split_pool.tile([P, SPLIT_BANKS * BANK], F32, tag="split", name="split", align_bytes=64)
+            source = raw[r][:].bitcast(F32)[:, 0 : SPLIT_BANKS * BANK]
             nc.vector.tensor_copy(
                 out=split[r][:].rearrange("p (u m i) -> p m u i", u=2, i=4),
                 in_=source.rearrange("p (m i u) -> p m u i", u=2, i=4),
@@ -104,8 +105,8 @@ def tile_simpa_pb_t_kernel(tc, A_p, x_p, w_p, out):
                 bank = transpose_psum.tile([P, BANK], F32, tag="bank", name="bank")
                 for u in range(2):
                     for c in range(2 * b, 2 * b + 2):
-                        if b < 2:
-                            words = split[r][:, (4 * u + c) * P : (4 * u + c + 1) * P]
+                        if b < SPLIT_BANKS:
+                            words = split[r][:, (2 * SPLIT_BANKS * u + c) * P : (2 * SPLIT_BANKS * u + c + 1) * P]
                         else:
                             words = raw[r][:].bitcast(F32)[:, c * 2 * P + u : (c + 1) * 2 * P : 2]
                         position = (2 * u + c % 2) * P
@@ -116,10 +117,7 @@ def tile_simpa_pb_t_kernel(tc, A_p, x_p, w_p, out):
                 target = grouped[(r, half)][:].bitcast(F32)[:, (b % 2) * BANK : (b % 2 + 1) * BANK]
                 target = target.rearrange("p (m i u) -> p m u i", i=2, u=2)
                 source = bank[:].rearrange("p (u m i) -> p m u i", u=2, i=2)
-                if b == 3 and r % 2 == 1:
-                    nc.vector.tensor_copy(out=target, in_=source)
-                else:
-                    nc.scalar.copy(out=target, in_=source)
+                nc.scalar.copy(out=target, in_=source)
                 if b == 0 and r + 1 < ROW_TILES:
                     split_words(r + 1)
                 if r == 0 and b in (1, 2):

from contextlib import ExitStack

import concourse.masks as masks
import concourse.mybir as mybir

F32 = mybir.dt.float32
BF16 = mybir.dt.bfloat16
U32 = mybir.dt.uint32
U8 = mybir.dt.uint8
FP8X4 = mybir.dt.float8_e4m3fn_x4
ALU = mybir.AluOpType
ACT = mybir.ActivationFunctionType

P = 128
NODES = 4096
FEATURES = 128
PASSES = NODES // (4 * P)
ROW_TILES = NODES // P
PAIRS = ROW_TILES // 2
BANK = 512
TILE_WORDS = PASSES * P
TRANSPOSE_BANKS = 6
SPLIT_BANKS = 3
RAW_TILES = 4
FLOPS = 2 * 2 * NODES * NODES * FEATURES


def h1_groups_ready(r):
    return max(0, (r - 2) // 4)


def tile_simpa_pb_t_kernel(tc, A_p, x_p, w_p, out):
    nc = tc.nc
    a_row_tiles = A_p.rearrange("(g m t) k -> g t m k", m=P, t=4)
    out_groups = out.rearrange("(g m t) d -> g m (t d)", m=P, t=4)

    with ExitStack() as ctx:
        keep = ctx.enter_context(tc.tile_pool(name="keep", bufs=1))
        raw_pool = ctx.enter_context(tc.tile_pool(name="raw_pool", bufs=RAW_TILES))
        split_pool = ctx.enter_context(tc.tile_pool(name="split_pool", bufs=2))
        grouped_pool = ctx.enter_context(tc.tile_pool(name="grouped_pool", bufs=4))
        h1_pool = ctx.enter_context(tc.tile_pool(name="h1_pool", bufs=2))
        transpose_psum = ctx.enter_context(tc.psum_pool(name="transpose_psum", bufs=TRANSPOSE_BANKS))
        product_psum = ctx.enter_context(tc.psum_pool(name="product_psum", bufs=2))
        ctx.enter_context(tc.manual_schedule())

        a_codes = keep.tile([P, ROW_TILES * TILE_WORDS], U32, name="a_codes", align_bytes=64)
        a_scales = keep.tile([P, ROW_TILES // 4 * TILE_WORDS], U8, name="a_scales", align_bytes=64)
        xh_codes = keep.tile([P, PASSES * 2 * FEATURES], U32, name="xh_codes", align_bytes=64)
        xh_scales = keep.tile([P, PASSES * 2 * FEATURES], U8, name="xh_scales", align_bytes=64)
        feat = keep.tile([P, ROW_TILES * FEATURES], F32, name="feat")
        x_raw = keep.tile([P, ROW_TILES * FEATURES], BF16, name="x_raw")
        ident = keep.tile([P, P], F32, name="ident")
        w_bf16 = keep.tile([P, 3], BF16, name="w_bf16")
        w = keep.tile([P, 3], F32, name="w")
        raw = {}
        split = {}
        grouped = {}
        products = {}
        h1_grouped = {}
        hop2 = {}

        def a_plane(r, first, width):
            g = r // 4
            columns = ((g // 4) * 4 + r % 4) * TILE_WORDS + first
            return a_scales[4 * (g % 4) : P, columns : columns + width]

        def load(r, pieces):
            raw[r] = raw_pool.tile([P, NODES], BF16, tag="raw", name="raw")
            width = NODES // pieces
            for i in range(pieces):
                columns = slice(i * width, (i + 1) * width)
                nc.sync.dma_start(out=raw[r][:, columns], in_=a_row_tiles[r // 4][r % 4][:, columns])

        def split_words(r):
            split[r] = split_pool.tile([P, SPLIT_BANKS * BANK], F32, tag="split", name="split", align_bytes=64)
            source = raw[r][:].bitcast(F32)[:, 0 : SPLIT_BANKS * BANK]
            nc.vector.tensor_copy(
                out=split[r][:].rearrange("p (u m i) -> p m u i", u=2, i=4),
                in_=source.rearrange("p (m i u) -> p m u i", u=2, i=4),
            )

        def quantise_a(r, half):
            first = half * (TILE_WORDS // 2)
            nc.vector.quantize_mx(
                out=a_codes[:, r * TILE_WORDS + first : r * TILE_WORDS + first + TILE_WORDS // 2].bitcast(FP8X4),
                scales=a_plane(r, first, TILE_WORDS // 2),
                in_=grouped[(r, half)][:],
            )

        def mx_pass(acc, r, c, first, width, start):
            moving = slice(c * 2 * FEATURES + first, c * 2 * FEATURES + first + width)
            nc.tensor.matmul_mx(
                out=acc,
                lhsT=a_codes[:, r * TILE_WORDS + c * P : r * TILE_WORDS + (c + 1) * P].bitcast(FP8X4),
                lhsT_scale=a_plane(r, c * P, P),
                rhs=xh_codes[:, moving].bitcast(FP8X4),
                rhs_scale=xh_scales[:, moving],
                start=start,
                stop=(c == PASSES - 1),
            )

        def transposes(r):
            for b in range(4):
                bank = transpose_psum.tile([P, BANK], F32, tag="bank", name="bank")
                for u in range(2):
                    for c in range(2 * b, 2 * b + 2):
                        if b < SPLIT_BANKS:
                            words = split[r][:, (2 * SPLIT_BANKS * u + c) * P : (2 * SPLIT_BANKS * u + c + 1) * P]
                        else:
                            words = raw[r][:].bitcast(F32)[:, c * 2 * P + u : (c + 1) * 2 * P : 2]
                        position = (2 * u + c % 2) * P
                        nc.tensor.transpose(out=bank[:, position : position + P], in_=words, identity=ident[:])
                half = b // 2
                if b % 2 == 0:
                    grouped[(r, half)] = grouped_pool.tile([P, 4 * BANK], BF16, tag="grouped", name="grouped", align_bytes=64)
                target = grouped[(r, half)][:].bitcast(F32)[:, (b % 2) * BANK : (b % 2 + 1) * BANK]
                target = target.rearrange("p (m i u) -> p m u i", i=2, u=2)
                source = bank[:].rearrange("p (u m i) -> p m u i", u=2, i=2)
                nc.scalar.copy(out=target, in_=source)
                if b == 0 and r + 1 < ROW_TILES:
                    split_words(r + 1)
                if r == 0 and b in (1, 2):
                    quantise_x(b - 1)
                if b == 1 and r > 0:
                    quantise_a(r - 1, 1)
                if b == 3:
                    quantise_a(r, 0)
                if b == 1 and r % 2 == 0 and r >= 4:
                    round_h1((r - 4) // 2)
                    add_products((r - 4) // 2, 0)
                if b == 2 and r % 2 == 0 and r >= 4:
                    add_products((r - 4) // 2, 1)
                if b == 3 and r % 4 == 2 and r >= 6:
                    quantise_h1((r - 6) // 4)

        def hop1(r):
            if r % 2 == 0:
                products[r // 2] = product_psum.tile([P, BANK], F32, tag="products", name="products")
            for c in range(PASSES):
                width = 2 * FEATURES if c < h1_groups_ready(r) else FEATURES
                first = (r % 2) * 2 * FEATURES
                mx_pass(products[r // 2][:, first : first + width], r, c, 0, width, c == 0)

        def round_h1(pair):
            g = pair // 2
            u = pair % 2
            if u == 0:
                h1_grouped[g] = h1_pool.tile([P, 4 * FEATURES], BF16, tag="h1", name="h1", align_bytes=64)
            parts = products[pair][:].rearrange("p (e s d) -> p e s d", e=2, s=2)
            nc.scalar.copy(
                out=h1_grouped[g][:].rearrange("p (d t) -> p d t", t=4)[:, :, 2 * u : 2 * u + 2],
                in_=parts[:, :, 0, :].rearrange("p e d -> p d e"),
            )

        def add_products(pair, part):
            parts = products[pair][:].rearrange("p (e s d) -> p e s d", e=2, s=2)
            rows = feat[:, 2 * pair * FEATURES : (2 * pair + 2) * FEATURES].rearrange("p (e d) -> p e d", e=2)
            if part == 0:
                nc.vector.tensor_scalar_mul(out=rows, in0=parts[:, :, 0, :], scalar1=w[:, 1:2])
            elif h1_groups_ready(2 * pair) > 0:
                nc.vector.scalar_tensor_tensor(
                    out=rows,
                    in0=parts[:, :, 1, :],
                    scalar=w[:, 2:3],
                    in1=rows,
                    op0=ALU.mult,
                    op1=ALU.add,
                )

        def quantise_h1(g):
            columns = slice(g * 2 * FEATURES + FEATURES, (g + 1) * 2 * FEATURES)
            nc.vector.quantize_mx(
                out=xh_codes[:, columns].bitcast(FP8X4), scales=xh_scales[:, columns], in_=h1_grouped[g][:]
            )

        def hop2_passes(r, first_pass, last_pass):
            g = r // 4
            if g not in hop2:
                if g < TRANSPOSE_BANKS:
                    hop2[g] = transpose_psum.tile([P, BANK], F32, tag="bank", name="hop2")
                else:
                    hop2[g] = product_psum.tile([P, BANK], F32, tag="products", name="hop2")
            for c in range(first_pass, last_pass + 1):
                acc = hop2[g][:, (r % 4) * FEATURES : (r % 4 + 1) * FEATURES]
                mx_pass(acc, r, c, FEATURES, FEATURES, c == h1_groups_ready(r))

        x_grouped = {}

        def group_x(half):
            x_grouped[half] = grouped_pool.tile([P, 4 * BANK], BF16, tag="grouped", name="x_half", align_bytes=64)
            nc.vector.tensor_copy(
                out=x_grouped[half][:].rearrange("p (c d t) -> p c d t", c=4, t=4),
                in_=x_raw[:, half * 4 * BANK : (half + 1) * 4 * BANK].rearrange("p (c t d) -> p c d t", c=4, t=4),
            )

        def quantise_x(half):
            for c in range(4 * half, 4 * half + 4):
                columns = slice(c * 2 * FEATURES, c * 2 * FEATURES + FEATURES)
                nc.vector.quantize_mx(
                    out=xh_codes[:, columns].bitcast(FP8X4),
                    scales=xh_scales[:, columns],
                    in_=x_grouped[half][:, (c % 4) * BANK : (c % 4 + 1) * BANK],
                )

        def add_x(g):
            rows = feat[:, g * BANK : (g + 1) * BANK]
            nc.vector.scalar_tensor_tensor(
                out=rows, in0=x_raw[:, g * BANK : (g + 1) * BANK], scalar=w[:, 0:1], in1=rows, op0=ALU.mult, op1=ALU.add
            )

        load(0, 2)
        nc.sync.dma_start(
            out=x_raw[:].rearrange("p (c w) -> p c w", c=PASSES),
            in_=x_p.rearrange("(c m t) d -> m c (t d)", m=P, t=4),
        )
        for r in range(1, RAW_TILES):
            load(r, 1)
        masks.make_identity(nc, ident[:])
        split_words(0)
        group_x(0)
        group_x(1)

        for r in range(ROW_TILES):
            if r == 1:
                nc.scalar.dma_start(out=w_bf16[:], in_=w_p.rearrange("a b -> (a b)").partition_broadcast(P))
            transposes(r)
            if r == 2:
                nc.vector.tensor_copy(out=w[:], in_=w_bf16[:])
            if r + RAW_TILES < ROW_TILES:
                load(r + RAW_TILES, 1)
            if r >= 2:
                hop1(r - 2)
        quantise_a(ROW_TILES - 1, 1)

        round_h1(PAIRS - 2)
        add_products(PAIRS - 2, 0)
        add_products(PAIRS - 2, 1)
        for g in range(PASSES // 2):
            add_x(g)
        hop1(ROW_TILES - 2)
        for g in range(TRANSPOSE_BANKS // 2):
            hop2_passes(4 * g, h1_groups_ready(4 * g), PASSES - 2)
        hop1(ROW_TILES - 1)
        for g in range(TRANSPOSE_BANKS // 2, TRANSPOSE_BANKS):
            hop2_passes(4 * g, h1_groups_ready(4 * g), PASSES - 2)
        round_h1(PAIRS - 1)
        quantise_h1(PASSES - 1)
        add_products(PAIRS - 1, 0)
        add_products(PAIRS - 1, 1)
        for g in range(PASSES):
            for r in range(4 * g, 4 * g + 4):
                if r % 4 == 0 and g < TRANSPOSE_BANKS:
                    hop2_passes(r, PASSES - 1, PASSES - 1)
                else:
                    hop2_passes(r, h1_groups_ready(r), PASSES - 1)
            if g < PASSES // 2:
                add_x(PASSES // 2 + g)
            rows = feat[:, g * BANK : (g + 1) * BANK]
            nc.vector.scalar_tensor_tensor(
                out=rows, in0=hop2[g][:], scalar=w[:, 2:3], in1=rows, op0=ALU.mult, op1=ALU.add
            )
            nc.sync.dma_start(out=out_groups[g], in_=rows)
